import numpy as np
import ml_dtypes


def mxq(x, axis, fmt="e4m3"):
    dtype, down = {"e4m3": (ml_dtypes.float8_e4m3fn, 7), "e5m2": (ml_dtypes.float8_e5m2, 14)}[fmt]
    v = np.moveaxis(np.asarray(x, np.float32).astype(ml_dtypes.bfloat16).astype(np.float64), axis, -1)
    blocks = v.reshape(v.shape[:-1] + (-1, 32))
    amax = np.abs(blocks).max(-1, keepdims=True)
    byte = np.maximum(np.where(amax > 0, np.frexp(amax)[1] - 1 + 127, 0) - down, 1)
    scale = np.exp2(byte - 127.0)
    codes = (blocks / scale).astype(np.float32).astype(dtype).astype(np.float64)
    return np.moveaxis((codes * scale).reshape(v.shape), -1, axis)


WIDE = False


def mx_kscale(k):
    if not WIDE:
        return np.ones(k)
    levels = np.array([10, -10, 5, -5, 0])
    if k % 512:
        return np.exp2(np.random.permutation(np.resize(levels, k // 32))).repeat(32)
    a = np.empty((k // 512, 16))
    for p in range(k // 512):
        a[p, :8] = np.random.permutation(np.resize(levels, 8))
        for g in range(8):
            far = levels[np.abs(levels - a[p, g]) >= 10]
            a[p, g + 8] = far[np.random.randint(len(far))]
    return np.exp2(a.ravel()).repeat(32)


BF16 = ml_dtypes.bfloat16


def bf(x):
    return np.asarray(x, np.float32).astype(BF16)


def f64(x):
    return np.asarray(x).astype(np.float64)


N, L, WD, C, O = 128, 64, 512, 512, 512
EPS = 1e-8
CONV_CLAMP = 256.0
ACT_GAIN = np.sqrt(2.0)
LRELU_SLOPE = 0.2
STYLE_WSCALE = 1.0 / np.sqrt(WD)
X_AMP = CONV_CLAMP / 2.0
W_AMP = np.sqrt(EPS)


def setup_inputs():
    s, t = mx_kscale(WD), mx_kscale(C)
    return {"x": bf(np.random.standard_normal((N, L, C)) * X_AMP),
            "w": bf(np.random.standard_normal((N, WD)) * s),
            "weight": bf(np.random.standard_normal((O, C)) * W_AMP / np.sqrt(C) / t[None, :]),
            "style_w": bf(np.random.standard_normal((C, WD)) * t[:, None] / s[None, :]),
            "style_b": bf((1.0 + 0.1 * np.random.standard_normal(C)) * t),
            "bias": bf(np.random.standard_normal(O) * 0.2 * X_AMP)}


def reference(x, w, weight, style_w, style_b, bias):
    wt = f64(weight)
    style = (mxq(f64(w), 1, "e4m3") @ mxq(f64(style_w), 1, "e4m3").T) * STYLE_WSCALE + f64(style_b)
    d = mxq(np.square(style), 1, "e4m3") @ mxq(np.square(wt), 1, "e4m3").T
    decoef = 1.0 / np.sqrt(d + EPS)
    x_mod = f64(x) * style[:, None, :]
    y = mxq(x_mod, 2, "e4m3") @ mxq(wt, 1, "e4m3").T
    y = y * decoef[:, None, :]
    y = y + f64(bias)
    y = np.where(y >= 0, y, LRELU_SLOPE * y) * ACT_GAIN
    return np.clip(y, -CONV_CLAMP, CONV_CLAMP)

@@ -1,0 +1,274 @@
+from contextlib import ExitStack
+import math
+
+import concourse.mybir as mybir
+from concourse.masks import make_identity
+
+F32 = mybir.dt.float32
+BF16 = mybir.dt.bfloat16
+U32 = mybir.dt.uint32
+U8 = mybir.dt.uint8
+FP8X4 = mybir.dt.float8_e4m3fn_x4
+ALU = mybir.AluOpType
+ACT = mybir.ActivationFunctionType
+
+P = 128
+NS, L, WD, C, O = 128, 64, 512, 512, 512
+EPS = 1e-8
+CLAMP = 256.0
+SLOPE = 0.2
+GAIN = math.sqrt(2.0)
+WSCALE = 1.0 / math.sqrt(WD)
+BANK_DT = F32
+
+NG = 16
+NSLOT = 4 * NG
+TAIL_ON_VECTOR = (57, 59, 61, 63)
+
+FLOPS = 2 * NS * L * C * O + 2 * NS * WD * C + 2 * NS * C * O
+
+
+def tile_modulatemlp_pa_kernel(tc, x, w, weight, style_w, style_b, bias, out):
+    nc = tc.nc
+    x_v = x.flatten_outer_dims().rearrange("(g q r) c -> g q (r c)", q=P, r=4)
+    out_v = out.flatten_outer_dims().rearrange("(g q r) o -> g q r o", q=P, r=4)
+
+    with ExitStack() as ctx:
+        const = ctx.enter_context(tc.tile_pool(name="const", bufs=1))
+        xin = ctx.enter_context(tc.tile_pool(name="xin", bufs=NG))
+        work = ctx.enter_context(tc.tile_pool(name="work", bufs=3))
+        ps_xt = ctx.enter_context(tc.psum_pool(name="ps_xt", bufs=2))
+        ps_mx = ctx.enter_context(tc.psum_pool(name="ps_mx", bufs=2))
+        ps_bt = ctx.enter_context(tc.psum_pool(name="ps_bt", bufs=4))
+
+        w_sb = const.tile([P, WD], BF16, name="w_sb")
+        nc.sync.dma_start(out=w_sb[:], in_=w)
+        sw_sb = const.tile([P, 4, WD], BF16, name="sw_sb")
+        sw_v = style_w.rearrange("(m t) k -> m t k", t=4)
+        nc.sync.dma_start(out=sw_sb[:, 0:2, :], in_=sw_v[:, 0:2, :])
+        nc.sync.dma_start(out=sw_sb[:, 2:4, :], in_=sw_v[:, 2:4, :])
+        sb4 = const.tile([P, 4], BF16, name="sb4")
+        nc.scalar.dma_start(out=sb4[:], in_=style_b.rearrange("(p t) -> p t", t=4))
+        bias4 = const.tile([P, 4], BF16, name="bias4")
+        with nc.allow_non_contiguous_dma(reason="512 bias values, one to a partition and tile"):
+            nc.scalar.dma_start(out=bias4[:], in_=bias.rearrange("(j p) -> p j", j=4))
+        xs = []
+        wt_sb = const.tile([P, 4, C], BF16, name="wt_sb")
+        for g in range(NG):
+            xg = xin.tile([P, 4 * C], BF16, name="xg", tag="xg")
+            nc.sync.dma_start(out=xg[:], in_=x_v[g])
+            xs.append(xg)
+            if g == 1:
+                nc.sync.dma_start(out=wt_sb[:], in_=weight.rearrange("(j m) c -> m j c", j=4))
+
+        ident = const.tile([P, P], F32, name="ident")
+        make_identity(nc, ident[:])
+
+        one = const.tile([P, 1], F32, name="one")
+        nc.vector.memset(one[:], 1.0)
+        warm = const.tile([P, 1], F32, name="warm")
+        nc.scalar.activation(out=warm[:], in_=one[:], func=ACT.Abs_reciprocal_sqrt)
+
+        def turn(bank_slot, rows_bf16):
+            words = rows_bf16.bitcast(F32)
+            for u in range(2):
+                nc.tensor.transpose(bank_slot[:, u, :], words[:, u:256:2], ident[:])
+
+        def quant(name, grp, width):
+            codes = const.tile([P, width // 4], U32, name=name + "_codes", align_bytes=64)
+            scl = const.tile([P, width // 4], U8, name=name + "_scl", align_bytes=64)
+            return codes, scl
+
+        def mx(out_ap, a, a_cols, b, b_cols):
+            nc.tensor.matmul_mx(
+                out=out_ap,
+                lhsT=a[0][:, a_cols].bitcast(FP8X4), lhsT_scale=a[1][:, a_cols],
+                rhs=b[0][:, b_cols].bitcast(FP8X4), rhs_scale=b[1][:, b_cols],
+                start=True, stop=True,
+            )
+
+        wT = ps_mx.tile([P, 2, P], F32, name="wT", tag="mx")
+        turn(wT, w_sb[:])
+        swT = []
+        for h in range(2):
+            t_ = ps_bt.tile([P, 2, 2, P], F32, name="swT", tag="bt")
+            for t2 in range(2):
+                turn(t_[:, t2], sw_sb[:, 2 * h + t2, :])
+            swT.append(t_)
+
+        w_grp = const.tile([P, 4 * NS], BF16, name="w_grp", align_bytes=64)
+        nc.vector.tensor_copy(
+            out=w_grp[:].bitcast(F32).rearrange("p (n u) -> p n u", u=2),
+            in_=wT[:].rearrange("p u n -> p n u"),
+        )
+        sw_grp = const.tile([P, 4 * C], BF16, name="sw_grp", align_bytes=64)
+        for h in range(2):
+            dst = sw_grp[:, 1024 * h:1024 * (h + 1)].bitcast(F32).rearrange("p (t m u) -> p t m u", t=2, u=2)
+            src = swT[h][:].rearrange("p t u m -> p t m u")
+            if h == 0:
+                nc.vector.tensor_copy(out=dst, in_=src)
+            else:
+                nc.scalar.copy(out=dst, in_=src)
+
+        xt = {}
+
+        def stage_T(g, h):
+            t_ = ps_xt.tile([P, 2, 2, P], F32, name="xt", tag="xt")
+            for r2 in range(2):
+                r = 2 * h + r2
+                turn(t_[:, r2], xs[g][:, C * r:C * (r + 1)])
+            xt[(g, h)] = t_
+
+        stage_T(0, 0)
+        stage_T(0, 1)
+
+        w_q = quant("w", w_grp, 4 * NS)
+        nc.vector.quantize_mx(out=w_q[0][:].bitcast(FP8X4), scales=w_q[1][:], in_=w_grp[:])
+        sw_q = quant("sw", sw_grp, 4 * C)
+        for h in range(2):
+            nc.vector.quantize_mx(
+                out=sw_q[0][:, 256 * h:256 * (h + 1)].bitcast(FP8X4),
+                scales=sw_q[1][:, 256 * h:256 * (h + 1)],
+                in_=sw_grp[:, 1024 * h:1024 * (h + 1)],
+            )
+
+        wt_grp = const.tile([P, 4 * O], BF16, name="wt_grp", align_bytes=64)
+        wsq_grp = const.tile([P, 4 * O], BF16, name="wsq_grp", align_bytes=64)
+        for h in range(2):
+            t_ = ps_bt.tile([P, 2, 2, P], F32, name="wtT", tag="bt")
+            for j2 in range(2):
+                turn(t_[:, j2], wt_sb[:, 2 * h + j2, :])
+            half = slice(1024 * h, 1024 * (h + 1))
+            nc.scalar.copy(
+                out=wt_grp[:, half].bitcast(F32).rearrange("p (j m u) -> p j m u", j=2, u=2),
+                in_=t_[:].rearrange("p j u m -> p j m u"),
+            )
+            nc.scalar.activation(out=wsq_grp[:, half], in_=wt_grp[:, half], func=ACT.Square)
+
+        s_bank = ps_mx.tile([P, 4, P], BANK_DT, name="s_bank", tag="mx")
+        for t in range(4):
+            mx(s_bank[:, t, :], sw_q, slice(P * t, P * (t + 1)), w_q, slice(0, NS))
+        style = const.tile([P, NS, 4], F32, name="style")
+        nc.vector.scalar_tensor_tensor(
+            out=style[:], in0=s_bank[:].rearrange("p t n -> p n t"), scalar=WSCALE,
+            in1=sb4[:].unsqueeze(1).to_broadcast([P, NS, 4]), op0=ALU.mult, op1=ALU.add,
+        )
+        ssq_grp = const.tile([P, 4 * NS], BF16, name="ssq_grp", align_bytes=64)
+        nc.scalar.activation(out=ssq_grp[:], in_=style[:].rearrange("p n t -> p (n t)"), func=ACT.Square)
+
+        wt_q = quant("wt", wt_grp, 4 * O)
+        wsq_q = quant("wsq", wsq_grp, 4 * O)
+        ssq_q = quant("ssq", ssq_grp, 4 * NS)
+        b_col = const.tile([P, 4], F32, name="b_col")
+        root = const.tile([P, 4, NS], F32, name="root")
+        dco = []
+
+        def demod_matmul():
+            d_bank = ps_bt.tile([P, 4, NS], F32, name="d_bank", tag="bt")
+            for j in range(4):
+                mx(d_bank[:, j, :], wsq_q, slice(P * j, P * (j + 1)), ssq_q, slice(0, NS))
+            nc.scalar.activation(out=root[:], in_=d_bank[:], func=ACT.Abs_reciprocal_sqrt, scale=0.5, bias=0.5 * EPS)
+
+        def demod_chunk(k):
+            t_ = const.tile([P, 4, 16], F32, name="dco%d" % k)
+            nc.vector.reciprocal(out=t_[:], in_=root[:, :, 16 * k:16 * (k + 1)])
+            dco.append(t_)
+
+        grp, xq, mxb, vt, ct, zt, btb, og = {}, {}, {}, {}, {}, {}, {}, {}
+
+        def stage_A(g, r):
+            if r == 0:
+                grp[g] = work.tile([P, 4 * 512], BF16, name="grp", tag="grp", bufs=2, align_bytes=64)
+            src = xt[(g, r // 2)][:, r % 2].bitcast(BF16).rearrange("p u (a b e) -> p a b u e", a=8, e=2)
+            sty = style[:, 8 * g:8 * (g + 1), :].unsqueeze(2).to_broadcast([P, 8, 16, 4])
+            nc.vector.tensor_tensor(
+                out=grp[g][:, 512 * r:512 * (r + 1)].rearrange("p (a b u e) -> p a b u e", a=8, u=2, e=2),
+                in0=src, in1=sty.rearrange("p a b (u e) -> p a b u e", u=2), op=ALU.mult,
+            )
+
+        def stage_Q(g):
+            codes = work.tile([P, 512], U32, name="xcodes", tag="xcodes", align_bytes=64)
+            scl = work.tile([P, 512], U8, name="xscl", tag="xscl", align_bytes=64)
+            nc.vector.quantize_mx(out=codes[:].bitcast(FP8X4), scales=scl[:], in_=grp[g][:])
+            xq[g] = (codes, scl)
+
+        def stage_M(g, j):
+            t_ = ps_mx.tile([P, 512], F32, name="mxb", tag="mx")
+            mx(t_[:], wt_q, slice(P * j, P * (j + 1)), xq[g], slice(0, 512))
+            mxb[(g, j)] = t_
+
+        def stage_E(g, j):
+            v = work.tile([P, 512], F32, name="v", tag="v", bufs=4)
+            src = mxb[(g, j)][:].rearrange("p (r a b) -> p a r b", r=4, a=8)
+            dst = v[:].rearrange("p (r a b) -> p a r b", r=4, a=8)
+            for a in range(8):
+                n = 8 * g + a
+                if 4 * g + j in TAIL_ON_VECTOR:
+                    nc.vector.tensor_scalar(out=dst[:, a], in0=src[:, a], scalar1=root[:, j, n:n + 1],
+                                            scalar2=b_col[:, j:j + 1], op0=ALU.mult, op1=ALU.add)
+                else:
+                    nc.scalar.activation(
+                        out=dst[:, a], in_=src[:, a], func=ACT.Identity,
+                        scale=root[:, j, n:n + 1], bias=b_col[:, j:j + 1],
+                    )
+            vt[(g, j)] = v
+
+        def stage_C(g, j):
+            c = work.tile([P, 512], F32, name="c", tag="c")
+            nc.gpsimd.tensor_scalar(out=c[:], in0=vt[(g, j)][:], scalar1=CLAMP, scalar2=-CLAMP / SLOPE,
+                                    op0=ALU.min, op1=ALU.max)
+            ct[(g, j)] = c
+
+        def stage_Z(g, j):
+            if j == 0:
+                og[g] = work.tile([P, 4, O], F32, name="og", tag="og")
+            nc.vector.scalar_tensor_tensor(out=og[g][:, :, P * j:P * (j + 1)], in0=btb[(g, j)][:], scalar=SLOPE,
+                                           in1=zt[(g, j)][:], op0=ALU.mult, op1=ALU.max)
+            if g == NG - 1:
+                nc.sync.dma_start(out=out_v[g][:, :, P * j:P * (j + 1)], in_=og[g][:, :, P * j:P * (j + 1)])
+            elif j == 3:
+                nc.sync.dma_start(out=out_v[g], in_=og[g][:])
+
+        def stage_B(g, j):
+            t_ = ps_bt.tile([P, 4, P], F32, name="btb", tag="bt")
+            for r in range(4):
+                nc.tensor.transpose(t_[:, r, :], ct[(g, j)][:, P * r:P * (r + 1)], ident[:])
+            btb[(g, j)] = t_
+
+        def stage_O(g, j):
+            cs = work.tile([P, 4, P], F32, name="cs", tag="cs")
+            nc.scalar.copy(out=cs[:], in_=btb[(g, j)][:])
+            zt[(g, j)] = cs
+
+        def ok(i):
+            return 0 <= i < NSLOT
+
+        for s in range(-8, NSLOT + 5):
+            if ok(s + 1):
+                stage_M((s + 1) // 4, (s + 1) % 4)
+            if ok(s - 2):
+                stage_B((s - 2) // 4, (s - 2) % 4)
+            if (s + 10) % 4 == 0 and 1 <= (s + 10) // 4 < NG:
+                stage_T((s + 10) // 4, 0)
+            if (s + 8) % 4 == 0 and 1 <= (s + 8) // 4 < NG:
+                stage_T((s + 8) // 4, 1)
+            if ok(s):
+                stage_E(s // 4, s % 4)
+            if ok(s - 3):
+                stage_O((s - 3) // 4, (s - 3) % 4)
+            if ok(s - 1):
+                stage_C((s - 1) // 4, (s - 1) % 4)
+            if ok(s + 8):
+                stage_A((s + 8) // 4, (s + 8) % 4)
+            if s == -7:
+                nc.vector.quantize_mx(out=wt_q[0][:].bitcast(FP8X4), scales=wt_q[1][:], in_=wt_grp[:])
+            if s == -6:
+                nc.vector.quantize_mx(out=ssq_q[0][:].bitcast(FP8X4), scales=ssq_q[1][:], in_=ssq_grp[:])
+            if s == -5:
+                nc.vector.quantize_mx(out=wsq_q[0][:].bitcast(FP8X4), scales=wsq_q[1][:], in_=wsq_grp[:])
+                demod_matmul()
+                nc.vector.tensor_scalar(out=b_col[:], in0=bias4[:], scalar1=GAIN, scalar2=None, op0=ALU.mult)
+            if s % 4 == 0 and 0 <= s // 4 + 1 < NG:
+                stage_Q(s // 4 + 1)
+            if ok(s - 4):
+                stage_Z((s - 4) // 4, (s - 4) % 4)

@@ -23,9 +23,14 @@ BANK_DT = F32
 
 NG = 16
 NSLOT = 4 * NG
-TAIL_ON_VECTOR = (57, 59, 61, 63)
+TAIL_ON_VECTOR = ()
+EVAC_ON_SCALAR = ()
 
 FLOPS = 2 * NS * L * C * O + 2 * NS * WD * C + 2 * NS * C * O
+
+
+def summed(s):
+    return s % 3 == 1
 
 
 def tile_modulatemlp_pa_kernel(tc, x, w, weight, style_w, style_b, bias, out):
@@ -38,8 +43,10 @@ def tile_modulatemlp_pa_kernel(tc, x, w, weight, style_w, style_b, bias, out):
         xin = ctx.enter_context(tc.tile_pool(name="xin", bufs=NG))
         work = ctx.enter_context(tc.tile_pool(name="work", bufs=3))
         ps_xt = ctx.enter_context(tc.psum_pool(name="ps_xt", bufs=2))
-        ps_mx = ctx.enter_context(tc.psum_pool(name="ps_mx", bufs=2))
-        ps_bt = ctx.enter_context(tc.psum_pool(name="ps_bt", bufs=4))
+        ps_mx = ctx.enter_context(tc.psum_pool(name="ps_mx", bufs=3))
+        ps_bt = ctx.enter_context(tc.psum_pool(name="ps_bt", bufs=3))
+
+        ctx.enter_context(tc.manual_schedule())
 
         w_sb = const.tile([P, WD], BF16, name="w_sb")
         nc.sync.dma_start(out=w_sb[:], in_=w)
@@ -58,8 +65,14 @@ def tile_modulatemlp_pa_kernel(tc, x, w, weight, style_w, style_b, bias, out):
             xg = xin.tile([P, 4 * C], BF16, name="xg", tag="xg")
             nc.sync.dma_start(out=xg[:], in_=x_v[g])
             xs.append(xg)
-            if g == 1:
+            if g == 0:
                 nc.sync.dma_start(out=wt_sb[:], in_=weight.rearrange("(j m) c -> m j c", j=4))
+
+        zero = const.tile([P, 512], BF16, name="zero")
+        nc.vector.memset(zero[:], 0.0)
+        idle = ps_mx.tile([P, 512], F32, name="idle", tag="mx")
+        for i in range(4):
+            nc.tensor.matmul(out=idle[:], lhsT=zero[:, 0:P], rhs=zero[:], start=True, stop=True)
 
         ident = const.tile([P, P], F32, name="ident")
         make_identity(nc, ident[:])
@@ -74,10 +87,13 @@ def tile_modulatemlp_pa_kernel(tc, x, w, weight, style_w, style_b, bias, out):
             for u in range(2):
                 nc.tensor.transpose(bank_slot[:, u, :], words[:, u:256:2], ident[:])
 
-        def quant(name, grp, width):
+        def quant_tiles(name, width):
             codes = const.tile([P, width // 4], U32, name=name + "_codes", align_bytes=64)
             scl = const.tile([P, width // 4], U8, name=name + "_scl", align_bytes=64)
             return codes, scl
+
+        def quantize(q, grp_ap, cols):
+            nc.vector.quantize_mx(out=q[0][:, cols].bitcast(FP8X4), scales=q[1][:, cols], in_=grp_ap)
 
         def mx(out_ap, a, a_cols, b, b_cols):
             nc.tensor.matmul_mx(
@@ -86,29 +102,6 @@ def tile_modulatemlp_pa_kernel(tc, x, w, weight, style_w, style_b, bias, out):
                 rhs=b[0][:, b_cols].bitcast(FP8X4), rhs_scale=b[1][:, b_cols],
                 start=True, stop=True,
             )
-
-        wT = ps_mx.tile([P, 2, P], F32, name="wT", tag="mx")
-        turn(wT, w_sb[:])
-        swT = []
-        for h in range(2):
-            t_ = ps_bt.tile([P, 2, 2, P], F32, name="swT", tag="bt")
-            for t2 in range(2):
-                turn(t_[:, t2], sw_sb[:, 2 * h + t2, :])
-            swT.append(t_)
-
-        w_grp = const.tile([P, 4 * NS], BF16, name="w_grp", align_bytes=64)
-        nc.vector.tensor_copy(
-            out=w_grp[:].bitcast(F32).rearrange("p (n u) -> p n u", u=2),
-            in_=wT[:].rearrange("p u n -> p n u"),
-        )
-        sw_grp = const.tile([P, 4 * C], BF16, name="sw_grp", align_bytes=64)
-        for h in range(2):
-            dst = sw_grp[:, 1024 * h:1024 * (h + 1)].bitcast(F32).rearrange("p (t m u) -> p t m u", t=2, u=2)
-            src = swT[h][:].rearrange("p t u m -> p t m u")
-            if h == 0:
-                nc.vector.tensor_copy(out=dst, in_=src)
-            else:
-                nc.scalar.copy(out=dst, in_=src)
 
         xt = {}
 
@@ -119,31 +112,30 @@ def tile_modulatemlp_pa_kernel(tc, x, w, weight, style_w, style_b, bias, out):
                 turn(t_[:, r2], xs[g][:, C * r:C * (r + 1)])
             xt[(g, h)] = t_
 
-        stage_T(0, 0)
-        stage_T(0, 1)
-
-        w_q = quant("w", w_grp, 4 * NS)
-        nc.vector.quantize_mx(out=w_q[0][:].bitcast(FP8X4), scales=w_q[1][:], in_=w_grp[:])
-        sw_q = quant("sw", sw_grp, 4 * C)
+        wT = ps_mx.tile([P, 2, P], F32, name="wT", tag="mx")
+        turn(wT, w_sb[:])
+        w_grp = const.tile([P, 4 * NS], BF16, name="w_grp", align_bytes=64)
+        nc.vector.tensor_copy(
+            out=w_grp[:].bitcast(F32).rearrange("p (n u) -> p n u", u=2),
+            in_=wT[:].rearrange("p u n -> p n u"),
+        )
+        sw_grp = const.tile([P, 4 * C], BF16, name="sw_grp", align_bytes=64)
         for h in range(2):
-            nc.vector.quantize_mx(
-                out=sw_q[0][:, 256 * h:256 * (h + 1)].bitcast(FP8X4),
-                scales=sw_q[1][:, 256 * h:256 * (h + 1)],
-                in_=sw_grp[:, 1024 * h:1024 * (h + 1)],
-            )
+            t_ = ps_bt.tile([P, 2, 2, P], F32, name="swT", tag="bt")
+            for t2 in range(2):
+                turn(t_[:, t2], sw_sb[:, 2 * h + t2, :])
+            dst = sw_grp[:, 1024 * h:1024 * (h + 1)].bitcast(F32).rearrange("p (t m u) -> p t m u", t=2, u=2)
+            src = t_[:].rearrange("p t u m -> p t m u")
+            if h == 0:
+                nc.vector.tensor_copy(out=dst, in_=src)
+            else:
+                nc.scalar.copy(out=dst, in_=src)
 
-        wt_grp = const.tile([P, 4 * O], BF16, name="wt_grp", align_bytes=64)
-        wsq_grp = const.tile([P, 4 * O], BF16, name="wsq_grp", align_bytes=64)
+        w_q = quant_tiles("w", 4 * NS)
+        quantize(w_q, w_grp[:], slice(0, NS))
+        sw_q = quant_tiles("sw", 4 * C)
         for h in range(2):
-            t_ = ps_bt.tile([P, 2, 2, P], F32, name="wtT", tag="bt")
-            for j2 in range(2):
-                turn(t_[:, j2], wt_sb[:, 2 * h + j2, :])
-            half = slice(1024 * h, 1024 * (h + 1))
-            nc.scalar.copy(
-                out=wt_grp[:, half].bitcast(F32).rearrange("p (j m u) -> p j m u", j=2, u=2),
-                in_=t_[:].rearrange("p j u m -> p j m u"),
-            )
-            nc.scalar.activation(out=wsq_grp[:, half], in_=wt_grp[:, half], func=ACT.Square)
+            quantize(sw_q, sw_grp[:, 1024 * h:1024 * (h + 1)], slice(256 * h, 256 * (h + 1)))
 
         s_bank = ps_mx.tile([P, 4, P], BANK_DT, name="s_bank", tag="mx")
         for t in range(4):
@@ -153,28 +145,38 @@ def tile_modulatemlp_pa_kernel(tc, x, w, weight, style_w, style_b, bias, out):
             out=style[:], in0=s_bank[:].rearrange("p t n -> p n t"), scalar=WSCALE,
             in1=sb4[:].unsqueeze(1).to_broadcast([P, NS, 4]), op0=ALU.mult, op1=ALU.add,
         )
+        stage_T(0, 0)
+        stage_T(0, 1)
         ssq_grp = const.tile([P, 4 * NS], BF16, name="ssq_grp", align_bytes=64)
         nc.scalar.activation(out=ssq_grp[:], in_=style[:].rearrange("p n t -> p (n t)"), func=ACT.Square)
 
-        wt_q = quant("wt", wt_grp, 4 * O)
-        wsq_q = quant("wsq", wsq_grp, 4 * O)
-        ssq_q = quant("ssq", ssq_grp, 4 * NS)
-        b_col = const.tile([P, 4], F32, name="b_col")
-        root = const.tile([P, 4, NS], F32, name="root")
-        dco = []
+        wt_grp = const.tile([P, 4 * O], BF16, name="wt_grp", align_bytes=64)
+        wsq_grp = const.tile([P, 4 * O], BF16, name="wsq_grp", align_bytes=64)
+        for h in range(2):
+            t_ = ps_bt.tile([P, 2, 2, P], F32, name="wtT", tag="bt")
+            for j2 in range(2):
+                turn(t_[:, j2], wt_sb[:, 2 * h + j2, :])
+            nc.scalar.copy(
+                out=wt_grp[:, 1024 * h:1024 * (h + 1)].bitcast(F32).rearrange("p (j m u) -> p j m u", j=2, u=2),
+                in_=t_[:].rearrange("p j u m -> p j m u"),
+            )
+        for h in range(2):
+            half = slice(1024 * h, 1024 * (h + 1))
+            nc.scalar.activation(out=wsq_grp[:, half], in_=wt_grp[:, half], func=ACT.Square)
 
-        def demod_matmul():
-            d_bank = ps_bt.tile([P, 4, NS], F32, name="d_bank", tag="bt")
+        wt_q = quant_tiles("wt", 4 * O)
+        wsq_q = quant_tiles("wsq", 4 * O)
+        ssq_q = quant_tiles("ssq", 4 * NS)
+        b_col = const.tile([P, 4], F32, name="b_col")
+        dco = const.tile([P, 4, NS], F32, name="dco")
+
+        def demod():
+            d_bank = ps_mx.tile([P, 4, NS], F32, name="d_bank", tag="mx")
             for j in range(4):
                 mx(d_bank[:, j, :], wsq_q, slice(P * j, P * (j + 1)), ssq_q, slice(0, NS))
-            nc.scalar.activation(out=root[:], in_=d_bank[:], func=ACT.Abs_reciprocal_sqrt, scale=0.5, bias=0.5 * EPS)
+            nc.scalar.activation(out=dco[:], in_=d_bank[:], func=ACT.Abs_reciprocal_sqrt, scale=0.5, bias=0.5 * EPS)
 
-        def demod_chunk(k):
-            t_ = const.tile([P, 4, 16], F32, name="dco%d" % k)
-            nc.vector.reciprocal(out=t_[:], in_=root[:, :, 16 * k:16 * (k + 1)])
-            dco.append(t_)
-
-        grp, xq, mxb, vt, ct, zt, btb, og = {}, {}, {}, {}, {}, {}, {}, {}
+        grp, xq, mxb, vt, ct, cst, btb, og = {}, {}, {}, {}, {}, {}, {}, {}
 
         def stage_A(g, r):
             if r == 0:
@@ -189,86 +191,110 @@ def tile_modulatemlp_pa_kernel(tc, x, w, weight, style_w, style_b, bias, out):
         def stage_Q(g):
             codes = work.tile([P, 512], U32, name="xcodes", tag="xcodes", align_bytes=64)
             scl = work.tile([P, 512], U8, name="xscl", tag="xscl", align_bytes=64)
-            nc.vector.quantize_mx(out=codes[:].bitcast(FP8X4), scales=scl[:], in_=grp[g][:])
             xq[g] = (codes, scl)
+            quantize(xq[g], grp[g][:], slice(0, 512))
 
-        def stage_M(g, j):
+        def stage_M(s):
+            g, j = s // 4, s % 4
             t_ = ps_mx.tile([P, 512], F32, name="mxb", tag="mx")
             mx(t_[:], wt_q, slice(P * j, P * (j + 1)), xq[g], slice(0, 512))
-            mxb[(g, j)] = t_
+            mxb[s] = t_
 
-        def stage_E(g, j):
+        def stage_E(s):
+            g, j = s // 4, s % 4
             v = work.tile([P, 512], F32, name="v", tag="v", bufs=4)
-            src = mxb[(g, j)][:].rearrange("p (r a b) -> p a r b", r=4, a=8)
+            src = mxb[s][:].rearrange("p (r a b) -> p a r b", r=4, a=8)
             dst = v[:].rearrange("p (r a b) -> p a r b", r=4, a=8)
             for a in range(8):
                 n = 8 * g + a
-                if 4 * g + j in TAIL_ON_VECTOR:
-                    nc.vector.tensor_scalar(out=dst[:, a], in0=src[:, a], scalar1=root[:, j, n:n + 1],
+                if s in TAIL_ON_VECTOR:
+                    nc.vector.tensor_scalar(out=dst[:, a], in0=src[:, a], scalar1=dco[:, j, n:n + 1],
                                             scalar2=b_col[:, j:j + 1], op0=ALU.mult, op1=ALU.add)
                 else:
-                    nc.scalar.activation(
-                        out=dst[:, a], in_=src[:, a], func=ACT.Identity,
-                        scale=root[:, j, n:n + 1], bias=b_col[:, j:j + 1],
-                    )
-            vt[(g, j)] = v
+                    nc.scalar.activation(out=dst[:, a], in_=src[:, a], func=ACT.Identity,
+                                         scale=dco[:, j, n:n + 1], bias=b_col[:, j:j + 1])
+            vt[s] = v
 
-        def stage_C(g, j):
-            c = work.tile([P, 512], F32, name="c", tag="c")
-            nc.gpsimd.tensor_scalar(out=c[:], in0=vt[(g, j)][:], scalar1=CLAMP, scalar2=-CLAMP / SLOPE,
-                                    op0=ALU.min, op1=ALU.max)
-            ct[(g, j)] = c
+        def stage_C(s):
+            if summed(s):
+                pos = work.tile([P, 512], F32, name="pos", tag="pos")
+                nc.gpsimd.tensor_scalar(out=pos[:], in0=vt[s][:], scalar1=CLAMP, scalar2=0.0, op0=ALU.min, op1=ALU.max)
+                neg = work.tile([P, 512], F32, name="neg", tag="neg")
+                nc.gpsimd.tensor_scalar(out=neg[:], in0=vt[s][:], scalar1=0.0, scalar2=-CLAMP / SLOPE,
+                                        op0=ALU.min, op1=ALU.max)
+                low = work.tile([P, 512], F32, name="low", tag="low")
+                nc.gpsimd.tensor_scalar(out=low[:], in0=neg[:], scalar1=SLOPE, scalar2=0.0, op0=ALU.mult, op1=ALU.add)
+                ct[s] = (pos, low)
+            else:
+                c = work.tile([P, 512], F32, name="c", tag="c")
+                nc.gpsimd.tensor_scalar(out=c[:], in0=vt[s][:], scalar1=CLAMP, scalar2=-CLAMP / SLOPE,
+                                        op0=ALU.min, op1=ALU.max)
+                ct[s] = (c,)
 
-        def stage_Z(g, j):
+        def stage_B(s):
+            t_ = ps_bt.tile([P, 4, P], F32, name="btb", tag="bt")
+            parts = ct[s]
+            for r in range(4):
+                for i in range(len(parts)):
+                    nc.tensor.matmul(out=t_[:, r, :], lhsT=parts[i][:, P * r:P * (r + 1)], rhs=ident[:],
+                                     is_transpose=True, start=(i == 0), stop=(i == len(parts) - 1))
+            btb[s] = t_
+
+        def stage_O(s):
+            if not summed(s):
+                cs = work.tile([P, 4, P], F32, name="cs", tag="cs")
+                nc.scalar.copy(out=cs[:], in_=btb[s][:])
+                cst[s] = cs
+
+        def stage_Z(s):
+            g, j = s // 4, s % 4
             if j == 0:
                 og[g] = work.tile([P, 4, O], F32, name="og", tag="og")
-            nc.vector.scalar_tensor_tensor(out=og[g][:, :, P * j:P * (j + 1)], in0=btb[(g, j)][:], scalar=SLOPE,
-                                           in1=zt[(g, j)][:], op0=ALU.mult, op1=ALU.max)
-            if g == NG - 1:
-                nc.sync.dma_start(out=out_v[g][:, :, P * j:P * (j + 1)], in_=og[g][:, :, P * j:P * (j + 1)])
+            dst = og[g][:, :, P * j:P * (j + 1)]
+            if not summed(s):
+                nc.vector.scalar_tensor_tensor(out=dst, in0=btb[s][:], scalar=SLOPE, in1=cst[s][:],
+                                               op0=ALU.mult, op1=ALU.max)
+            elif s in EVAC_ON_SCALAR:
+                nc.scalar.copy(out=dst, in_=btb[s][:])
+            else:
+                nc.vector.tensor_copy(out=dst, in_=btb[s][:])
+            if g >= NG - 2:
+                nc.sync.dma_start(out=out_v[g][:, :, P * j:P * (j + 1)], in_=dst)
             elif j == 3:
                 nc.sync.dma_start(out=out_v[g], in_=og[g][:])
-
-        def stage_B(g, j):
-            t_ = ps_bt.tile([P, 4, P], F32, name="btb", tag="bt")
-            for r in range(4):
-                nc.tensor.transpose(t_[:, r, :], ct[(g, j)][:, P * r:P * (r + 1)], ident[:])
-            btb[(g, j)] = t_
-
-        def stage_O(g, j):
-            cs = work.tile([P, 4, P], F32, name="cs", tag="cs")
-            nc.scalar.copy(out=cs[:], in_=btb[(g, j)][:])
-            zt[(g, j)] = cs
 
         def ok(i):
             return 0 <= i < NSLOT
 
+
         for s in range(-8, NSLOT + 5):
-            if ok(s + 1):
-                stage_M((s + 1) // 4, (s + 1) % 4)
-            if ok(s - 2):
-                stage_B((s - 2) // 4, (s - 2) % 4)
             if (s + 10) % 4 == 0 and 1 <= (s + 10) // 4 < NG:
                 stage_T((s + 10) // 4, 0)
             if (s + 8) % 4 == 0 and 1 <= (s + 8) // 4 < NG:
                 stage_T((s + 8) // 4, 1)
+            if ok(s - 2):
+                stage_B(s - 2)
+            if s % 2 == 0:
+                for i in (s + 2, s + 3):
+                    if ok(i):
+                        stage_M(i)
             if ok(s):
-                stage_E(s // 4, s % 4)
+                stage_E(s)
             if ok(s - 3):
-                stage_O((s - 3) // 4, (s - 3) % 4)
+                stage_O(s - 3)
             if ok(s - 1):
-                stage_C((s - 1) // 4, (s - 1) % 4)
+                stage_C(s - 1)
             if ok(s + 8):
                 stage_A((s + 8) // 4, (s + 8) % 4)
             if s == -7:
-                nc.vector.quantize_mx(out=wt_q[0][:].bitcast(FP8X4), scales=wt_q[1][:], in_=wt_grp[:])
-            if s == -6:
-                nc.vector.quantize_mx(out=ssq_q[0][:].bitcast(FP8X4), scales=ssq_q[1][:], in_=ssq_grp[:])
-            if s == -5:
-                nc.vector.quantize_mx(out=wsq_q[0][:].bitcast(FP8X4), scales=wsq_q[1][:], in_=wsq_grp[:])
-                demod_matmul()
-                nc.vector.tensor_scalar(out=b_col[:], in0=bias4[:], scalar1=GAIN, scalar2=None, op0=ALU.mult)
+                quantize(ssq_q, ssq_grp[:], slice(0, NS))
+            if s == -4:
+                quantize(wt_q, wt_grp[:], slice(0, O))
             if s % 4 == 0 and 0 <= s // 4 + 1 < NG:
                 stage_Q(s // 4 + 1)
+            if s == -3:
+                quantize(wsq_q, wsq_grp[:], slice(0, O))
+                demod()
+                nc.vector.tensor_scalar(out=b_col[:], in0=bias4[:], scalar1=GAIN, scalar2=None, op0=ALU.mult)
             if ok(s - 4):
-                stage_Z((s - 4) // 4, (s - 4) % 4)
+                stage_Z(s - 4)

from contextlib import ExitStack
import math

import concourse.mybir as mybir
from concourse.masks import make_identity

F32 = mybir.dt.float32
BF16 = mybir.dt.bfloat16
U32 = mybir.dt.uint32
U8 = mybir.dt.uint8
FP8X4 = mybir.dt.float8_e4m3fn_x4
ALU = mybir.AluOpType
ACT = mybir.ActivationFunctionType

P = 128
NS, L, WD, C, O = 128, 64, 512, 512, 512
EPS = 1e-8
CLAMP = 256.0
SLOPE = 0.2
GAIN = math.sqrt(2.0)
WSCALE = 1.0 / math.sqrt(WD)
BANK_DT = F32

NG = 16
NSLOT = 4 * NG
TAIL_ON_VECTOR = ()
EVAC_ON_SCALAR = ()

FLOPS = 2 * NS * L * C * O + 2 * NS * WD * C + 2 * NS * C * O


def summed(s):
    return s % 3 == 1


def tile_modulatemlp_pa_kernel(tc, x, w, weight, style_w, style_b, bias, out):
    nc = tc.nc
    x_v = x.flatten_outer_dims().rearrange("(g q r) c -> g q (r c)", q=P, r=4)
    out_v = out.flatten_outer_dims().rearrange("(g q r) o -> g q r o", q=P, r=4)

    with ExitStack() as ctx:
        const = ctx.enter_context(tc.tile_pool(name="const", bufs=1))
        xin = ctx.enter_context(tc.tile_pool(name="xin", bufs=NG))
        work = ctx.enter_context(tc.tile_pool(name="work", bufs=3))
        ps_xt = ctx.enter_context(tc.psum_pool(name="ps_xt", bufs=2))
        ps_mx = ctx.enter_context(tc.psum_pool(name="ps_mx", bufs=3))
        ps_bt = ctx.enter_context(tc.psum_pool(name="ps_bt", bufs=3))

        ctx.enter_context(tc.manual_schedule())

        w_sb = const.tile([P, WD], BF16, name="w_sb")
        nc.sync.dma_start(out=w_sb[:], in_=w)
        sw_sb = const.tile([P, 4, WD], BF16, name="sw_sb")
        sw_v = style_w.rearrange("(m t) k -> m t k", t=4)
        nc.sync.dma_start(out=sw_sb[:, 0:2, :], in_=sw_v[:, 0:2, :])
        nc.sync.dma_start(out=sw_sb[:, 2:4, :], in_=sw_v[:, 2:4, :])
        sb4 = const.tile([P, 4], BF16, name="sb4")
        nc.scalar.dma_start(out=sb4[:], in_=style_b.rearrange("(p t) -> p t", t=4))
        bias4 = const.tile([P, 4], BF16, name="bias4")
        with nc.allow_non_contiguous_dma(reason="512 bias values, one to a partition and tile"):
            nc.scalar.dma_start(out=bias4[:], in_=bias.rearrange("(j p) -> p j", j=4))
        xs = []
        wt_sb = const.tile([P, 4, C], BF16, name="wt_sb")
        for g in range(NG):
            xg = xin.tile([P, 4 * C], BF16, name="xg", tag="xg")
            nc.sync.dma_start(out=xg[:], in_=x_v[g])
            xs.append(xg)
            if g == 0:
                nc.sync.dma_start(out=wt_sb[:], in_=weight.rearrange("(j m) c -> m j c", j=4))

        zero = const.tile([P, 512], BF16, name="zero")
        nc.vector.memset(zero[:], 0.0)
        idle = ps_mx.tile([P, 512], F32, name="idle", tag="mx")
        for i in range(4):
            nc.tensor.matmul(out=idle[:], lhsT=zero[:, 0:P], rhs=zero[:], start=True, stop=True)

        ident = const.tile([P, P], F32, name="ident")
        make_identity(nc, ident[:])

        one = const.tile([P, 1], F32, name="one")
        nc.vector.memset(one[:], 1.0)
        warm = const.tile([P, 1], F32, name="warm")
        nc.scalar.activation(out=warm[:], in_=one[:], func=ACT.Abs_reciprocal_sqrt)

        def turn(bank_slot, rows_bf16):
            words = rows_bf16.bitcast(F32)
            for u in range(2):
                nc.tensor.transpose(bank_slot[:, u, :], words[:, u:256:2], ident[:])

        def quant_tiles(name, width):
            codes = const.tile([P, width // 4], U32, name=name + "_codes", align_bytes=64)
            scl = const.tile([P, width // 4], U8, name=name + "_scl", align_bytes=64)
            return codes, scl

        def quantize(q, grp_ap, cols):
            nc.vector.quantize_mx(out=q[0][:, cols].bitcast(FP8X4), scales=q[1][:, cols], in_=grp_ap)

        def mx(out_ap, a, a_cols, b, b_cols):
            nc.tensor.matmul_mx(
                out=out_ap,
                lhsT=a[0][:, a_cols].bitcast(FP8X4), lhsT_scale=a[1][:, a_cols],
                rhs=b[0][:, b_cols].bitcast(FP8X4), rhs_scale=b[1][:, b_cols],
                start=True, stop=True,
            )

        xt = {}

        def stage_T(g, h):
            t_ = ps_xt.tile([P, 2, 2, P], F32, name="xt", tag="xt")
            for r2 in range(2):
                r = 2 * h + r2
                turn(t_[:, r2], xs[g][:, C * r:C * (r + 1)])
            xt[(g, h)] = t_

        wT = ps_mx.tile([P, 2, P], F32, name="wT", tag="mx")
        turn(wT, w_sb[:])
        w_grp = const.tile([P, 4 * NS], BF16, name="w_grp", align_bytes=64)
        nc.vector.tensor_copy(
            out=w_grp[:].bitcast(F32).rearrange("p (n u) -> p n u", u=2),
            in_=wT[:].rearrange("p u n -> p n u"),
        )
        sw_grp = const.tile([P, 4 * C], BF16, name="sw_grp", align_bytes=64)
        for h in range(2):
            t_ = ps_bt.tile([P, 2, 2, P], F32, name="swT", tag="bt")
            for t2 in range(2):
                turn(t_[:, t2], sw_sb[:, 2 * h + t2, :])
            dst = sw_grp[:, 1024 * h:1024 * (h + 1)].bitcast(F32).rearrange("p (t m u) -> p t m u", t=2, u=2)
            src = t_[:].rearrange("p t u m -> p t m u")
            if h == 0:
                nc.vector.tensor_copy(out=dst, in_=src)
            else:
                nc.scalar.copy(out=dst, in_=src)

        w_q = quant_tiles("w", 4 * NS)
        quantize(w_q, w_grp[:], slice(0, NS))
        sw_q = quant_tiles("sw", 4 * C)
        for h in range(2):
            quantize(sw_q, sw_grp[:, 1024 * h:1024 * (h + 1)], slice(256 * h, 256 * (h + 1)))

        s_bank = ps_mx.tile([P, 4, P], BANK_DT, name="s_bank", tag="mx")
        for t in range(4):
            mx(s_bank[:, t, :], sw_q, slice(P * t, P * (t + 1)), w_q, slice(0, NS))
        style = const.tile([P, NS, 4], F32, name="style")
        nc.vector.scalar_tensor_tensor(
            out=style[:], in0=s_bank[:].rearrange("p t n -> p n t"), scalar=WSCALE,
            in1=sb4[:].unsqueeze(1).to_broadcast([P, NS, 4]), op0=ALU.mult, op1=ALU.add,
        )
        stage_T(0, 0)
        stage_T(0, 1)
        ssq_grp = const.tile([P, 4 * NS], BF16, name="ssq_grp", align_bytes=64)
        nc.scalar.activation(out=ssq_grp[:], in_=style[:].rearrange("p n t -> p (n t)"), func=ACT.Square)

        wt_grp = const.tile([P, 4 * O], BF16, name="wt_grp", align_bytes=64)
        wsq_grp = const.tile([P, 4 * O], BF16, name="wsq_grp", align_bytes=64)
        for h in range(2):
            t_ = ps_bt.tile([P, 2, 2, P], F32, name="wtT", tag="bt")
            for j2 in range(2):
                turn(t_[:, j2], wt_sb[:, 2 * h + j2, :])
            nc.scalar.copy(
                out=wt_grp[:, 1024 * h:1024 * (h + 1)].bitcast(F32).rearrange("p (j m u) -> p j m u", j=2, u=2),
                in_=t_[:].rearrange("p j u m -> p j m u"),
            )
        for h in range(2):
            half = slice(1024 * h, 1024 * (h + 1))
            nc.scalar.activation(out=wsq_grp[:, half], in_=wt_grp[:, half], func=ACT.Square)

        wt_q = quant_tiles("wt", 4 * O)
        wsq_q = quant_tiles("wsq", 4 * O)
        ssq_q = quant_tiles("ssq", 4 * NS)
        b_col = const.tile([P, 4], F32, name="b_col")
        dco = const.tile([P, 4, NS], F32, name="dco")

        def demod():
            d_bank = ps_mx.tile([P, 4, NS], F32, name="d_bank", tag="mx")
            for j in range(4):
                mx(d_bank[:, j, :], wsq_q, slice(P * j, P * (j + 1)), ssq_q, slice(0, NS))
            nc.scalar.activation(out=dco[:], in_=d_bank[:], func=ACT.Abs_reciprocal_sqrt, scale=0.5, bias=0.5 * EPS)

        grp, xq, mxb, vt, ct, cst, btb, og = {}, {}, {}, {}, {}, {}, {}, {}

        def stage_A(g, r):
            if r == 0:
                grp[g] = work.tile([P, 4 * 512], BF16, name="grp", tag="grp", bufs=2, align_bytes=64)
            src = xt[(g, r // 2)][:, r % 2].bitcast(BF16).rearrange("p u (a b e) -> p a b u e", a=8, e=2)
            sty = style[:, 8 * g:8 * (g + 1), :].unsqueeze(2).to_broadcast([P, 8, 16, 4])
            nc.vector.tensor_tensor(
                out=grp[g][:, 512 * r:512 * (r + 1)].rearrange("p (a b u e) -> p a b u e", a=8, u=2, e=2),
                in0=src, in1=sty.rearrange("p a b (u e) -> p a b u e", u=2), op=ALU.mult,
            )

        def stage_Q(g):
            codes = work.tile([P, 512], U32, name="xcodes", tag="xcodes", align_bytes=64)
            scl = work.tile([P, 512], U8, name="xscl", tag="xscl", align_bytes=64)
            xq[g] = (codes, scl)
            quantize(xq[g], grp[g][:], slice(0, 512))

        def stage_M(s):
            g, j = s // 4, s % 4
            t_ = ps_mx.tile([P, 512], F32, name="mxb", tag="mx")
            mx(t_[:], wt_q, slice(P * j, P * (j + 1)), xq[g], slice(0, 512))
            mxb[s] = t_

        def stage_E(s):
            g, j = s // 4, s % 4
            v = work.tile([P, 512], F32, name="v", tag="v", bufs=4)
            src = mxb[s][:].rearrange("p (r a b) -> p a r b", r=4, a=8)
            dst = v[:].rearrange("p (r a b) -> p a r b", r=4, a=8)
            for a in range(8):
                n = 8 * g + a
                if s in TAIL_ON_VECTOR:
                    nc.vector.tensor_scalar(out=dst[:, a], in0=src[:, a], scalar1=dco[:, j, n:n + 1],
                                            scalar2=b_col[:, j:j + 1], op0=ALU.mult, op1=ALU.add)
                else:
                    nc.scalar.activation(out=dst[:, a], in_=src[:, a], func=ACT.Identity,
                                         scale=dco[:, j, n:n + 1], bias=b_col[:, j:j + 1])
            vt[s] = v

        def stage_C(s):
            if summed(s):
                pos = work.tile([P, 512], F32, name="pos", tag="pos")
                nc.gpsimd.tensor_scalar(out=pos[:], in0=vt[s][:], scalar1=CLAMP, scalar2=0.0, op0=ALU.min, op1=ALU.max)
                neg = work.tile([P, 512], F32, name="neg", tag="neg")
                nc.gpsimd.tensor_scalar(out=neg[:], in0=vt[s][:], scalar1=0.0, scalar2=-CLAMP / SLOPE,
                                        op0=ALU.min, op1=ALU.max)
                low = work.tile([P, 512], F32, name="low", tag="low")
                nc.gpsimd.tensor_scalar(out=low[:], in0=neg[:], scalar1=SLOPE, scalar2=0.0, op0=ALU.mult, op1=ALU.add)
                ct[s] = (pos, low)
            else:
                c = work.tile([P, 512], F32, name="c", tag="c")
                nc.gpsimd.tensor_scalar(out=c[:], in0=vt[s][:], scalar1=CLAMP, scalar2=-CLAMP / SLOPE,
                                        op0=ALU.min, op1=ALU.max)
                ct[s] = (c,)

        def stage_B(s):
            t_ = ps_bt.tile([P, 4, P], F32, name="btb", tag="bt")
            parts = ct[s]
            for r in range(4):
                for i in range(len(parts)):
                    nc.tensor.matmul(out=t_[:, r, :], lhsT=parts[i][:, P * r:P * (r + 1)], rhs=ident[:],
                                     is_transpose=True, start=(i == 0), stop=(i == len(parts) - 1))
            btb[s] = t_

        def stage_O(s):
            if not summed(s):
                cs = work.tile([P, 4, P], F32, name="cs", tag="cs")
                nc.scalar.copy(out=cs[:], in_=btb[s][:])
                cst[s] = cs

        def stage_Z(s):
            g, j = s // 4, s % 4
            if j == 0:
                og[g] = work.tile([P, 4, O], F32, name="og", tag="og")
            dst = og[g][:, :, P * j:P * (j + 1)]
            if not summed(s):
                nc.vector.scalar_tensor_tensor(out=dst, in0=btb[s][:], scalar=SLOPE, in1=cst[s][:],
                                               op0=ALU.mult, op1=ALU.max)
            elif s in EVAC_ON_SCALAR:
                nc.scalar.copy(out=dst, in_=btb[s][:])
            else:
                nc.vector.tensor_copy(out=dst, in_=btb[s][:])
            if g >= NG - 2:
                nc.sync.dma_start(out=out_v[g][:, :, P * j:P * (j + 1)], in_=dst)
            elif j == 3:
                nc.sync.dma_start(out=out_v[g], in_=og[g][:])

        def ok(i):
            return 0 <= i < NSLOT


        for s in range(-8, NSLOT + 5):
            if (s + 10) % 4 == 0 and 1 <= (s + 10) // 4 < NG:
                stage_T((s + 10) // 4, 0)
            if (s + 8) % 4 == 0 and 1 <= (s + 8) // 4 < NG:
                stage_T((s + 8) // 4, 1)
            if ok(s - 2):
                stage_B(s - 2)
            if s % 2 == 0:
                for i in (s + 2, s + 3):
                    if ok(i):
                        stage_M(i)
            if ok(s):
                stage_E(s)
            if ok(s - 3):
                stage_O(s - 3)
            if ok(s - 1):
                stage_C(s - 1)
            if ok(s + 8):
                stage_A((s + 8) // 4, (s + 8) % 4)
            if s == -7:
                quantize(ssq_q, ssq_grp[:], slice(0, NS))
            if s == -4:
                quantize(wt_q, wt_grp[:], slice(0, O))
            if s % 4 == 0 and 0 <= s // 4 + 1 < NG:
                stage_Q(s // 4 + 1)
            if s == -3:
                quantize(wsq_q, wsq_grp[:], slice(0, O))
                demod()
                nc.vector.tensor_scalar(out=b_col[:], in0=bias4[:], scalar1=GAIN, scalar2=None, op0=ALU.mult)
            if ok(s - 4):
                stage_Z(s - 4)
